import numpy as np
import ml_dtypes


def mxq(x, axis, fmt="e4m3"):
    dtype, down = {"e4m3": (ml_dtypes.float8_e4m3fn, 7), "e5m2": (ml_dtypes.float8_e5m2, 14)}[fmt]
    v = np.moveaxis(np.asarray(x, np.float32).astype(ml_dtypes.bfloat16).astype(np.float64), axis, -1)
    blocks = v.reshape(v.shape[:-1] + (-1, 32))
    amax = np.abs(blocks).max(-1, keepdims=True)
    byte = np.maximum(np.where(amax > 0, np.frexp(amax)[1] - 1 + 127, 0) - down, 1)
    scale = np.exp2(byte - 127.0)
    codes = (blocks / scale).astype(np.float32).astype(dtype).astype(np.float64)
    return np.moveaxis((codes * scale).reshape(v.shape), -1, axis)


WIDE = False


def mx_kscale(k):
    if not WIDE:
        return np.ones(k)
    levels = np.array([10, -10, 5, -5, 0])
    a = np.random.permutation(np.resize(levels, k // 512 * 4)).reshape(k // 512, 4)
    idx = np.arange(k)
    return np.exp2(a[idx // 512, idx % 128 // 32])


BF16 = ml_dtypes.bfloat16


def bf(x):
    return np.asarray(x, np.float32).astype(BF16)


def f64(x):
    return np.asarray(x).astype(np.float64)


B, DIN, DOUT = 1024, 2048, 2048

MIN_NORM = 1e-15
PROJ_EPS = 1e-3
W_MUL = 0.1
B_MUL = 0.1
C = 1.0


def artanh(x):
    x = np.clip(x, -1.0 + 1e-5, 1.0 - 1e-5)
    return 0.5 * (np.log1p(x) - np.log1p(-x))


def mobius_matvec(w, x, c):
    sqrt_c = c ** 0.5
    x_norm = np.maximum(np.linalg.norm(x, axis=-1, keepdims=True), MIN_NORM)
    mx = mxq(x, 1, "e4m3") @ mxq(w, 1, "e4m3").T
    mx_norm = np.maximum(np.linalg.norm(mx, axis=-1, keepdims=True), MIN_NORM)
    res = np.tanh(mx_norm / x_norm * artanh(sqrt_c * x_norm)) * mx / (mx_norm * sqrt_c)
    zero_row = np.all(mx == 0, axis=-1, keepdims=True)
    return np.where(zero_row, 0.0, res)


def expmap0(u, c):
    sqrt_c = c ** 0.5
    u_norm = np.maximum(np.linalg.norm(u, axis=-1, keepdims=True), MIN_NORM)
    return np.tanh(sqrt_c * u_norm) * u / (sqrt_c * u_norm)


def mobius_add(x, y, c):
    x2 = np.sum(x * x, axis=-1, keepdims=True)
    y2 = np.sum(y * y, axis=-1, keepdims=True)
    xy = np.sum(x * y, axis=-1, keepdims=True)
    num = (1 + 2 * c * xy + c * y2) * x + (1 - c * x2) * y
    denom = 1 + 2 * c * xy + c * c * x2 * y2
    return num / np.maximum(denom, MIN_NORM)


def project(x, c):
    sqrt_c = c ** 0.5
    norm = np.maximum(np.linalg.norm(x, axis=-1, keepdims=True), MIN_NORM)
    maxnorm = (1.0 - PROJ_EPS) / sqrt_c
    return np.where(norm > maxnorm, x / norm * maxnorm, x)


def setup_inputs():
    s = mx_kscale(DIN)
    g = np.exp2(np.ceil(np.log2(np.sqrt(np.mean(s * s)))))
    return {"x": bf(np.random.standard_normal((B, DIN)) * 0.7 / np.sqrt(DIN) * s / g),
            "weight": bf(np.random.standard_normal((DOUT, DIN)) * 10.0 / np.sqrt(DOUT) * g / s),
            "bias": bf(np.random.standard_normal(DOUT) * 3.0 / np.sqrt(DOUT))}


def reference(x, weight, bias):
    c = C
    w_lr = f64(weight) * W_MUL
    mv = mobius_matvec(w_lr, f64(x), c)
    b = expmap0(f64(bias) * B_MUL, c)
    out = project(mobius_add(mv, b[None, :], 1.0), c)
    return np.where(out >= 0, out, 0.2 * out)

from contextlib import ExitStack

import concourse.bass as bass
import concourse.mybir as mybir
import concourse.tile as tile
from concourse.masks import make_identity

F32 = mybir.dt.float32
BF16 = mybir.dt.bfloat16
U32 = mybir.dt.uint32
U8 = mybir.dt.uint8
FP8X4 = mybir.dt.float8_e4m3fn_x4
ALU = mybir.AluOpType
ACT = mybir.ActivationFunctionType
AX = mybir.AxisListType

P = 128
B, DIN, DOUT = 1024, 2048, 2048
FLOPS = 2 * B * DIN * DOUT
NG = DIN // 512
NT = B // P
NB = DOUT // 512
PINNED = False


def tile_hypequalizedlinear_kernel(tc, x, weight, bias, out):
    nc = tc.nc
    x_v = x.rearrange("(c a p) k -> c p a k", a=2, p=P)
    w_v = weight.rearrange("(c a p) k -> c p a k", a=2, p=P)
    out_v = out.rearrange("(t p) n -> t p n", p=P)

    with ExitStack() as ctx:
        if PINNED:
            ctx.enter_context(tc.manual_schedule())
        const = ctx.enter_context(tc.tile_pool(name="const", bufs=1))
        xin = ctx.enter_context(tc.tile_pool(name="xin", bufs=4))
        win = ctx.enter_context(tc.tile_pool(name="win", bufs=4))
        gxp = ctx.enter_context(tc.tile_pool(name="gxp", bufs=2))
        gwp = ctx.enter_context(tc.tile_pool(name="gwp", bufs=3))
        tpl = ctx.enter_context(tc.tile_pool(name="tpl", bufs=3))
        jkp = ctx.enter_context(tc.tile_pool(name="jkp", bufs=4))
        sm = ctx.enter_context(tc.tile_pool(name="sm", bufs=3))
        psum = ctx.enter_context(tc.psum_pool(name="psum", bufs=1))

        ident = const.tile([P, P], F32, name="ident")
        make_identity(nc, ident[:])
        mh8 = const.tile([P, 8], F32, name="mh8")
        nc.gpsimd.memset(mh8[:], -0.5)
        ex2 = const.tile([P, 2], F32, name="ex2")
        nc.gpsimd.memset(ex2[:, 0:1], -1.0)
        nc.gpsimd.memset(ex2[:, 1:2], -0.5)

        bias_bc = const.tile([P, DOUT], BF16, name="bias_bc")
        b_bc = const.tile([P, DOUT], F32, name="b_bc")
        xc = const.tile([P, 4, NG, 256], U32, name="xc", align_bytes=64)
        xs = const.tile([P, 4, NG, 256], U8, name="xs", align_bytes=64)
        wc = const.tile([P, NG, DOUT], U32, name="wc", align_bytes=64)
        ws = const.tile([P, NG, DOUT], U8, name="ws", align_bytes=64)
        xn2 = const.tile([P, NT], F32, name="xn2")
        q = const.tile([P, NT], F32, name="q")
        y2 = const.tile([P, 1], F32, name="y2")
        c2 = const.tile([P, 1], F32, name="c2")

        state = {"bank": 0}

        def transposes(src, g):
            bk = 4 + state["bank"] % 4
            state["bank"] += 1
            tp = psum.tile([P, 2, 2, P], F32, tag="bk%d" % bk, name="tp")
            words = src[:].bitcast(F32)
            for u in range(2):
                for a in range(2):
                    lo = 256 * g + 128 * u
                    nc.tensor.transpose(tp[:, u, a, :], words[:, a, lo:lo + 128], ident[:])
            return tp

        def x_pair(c, src):
            gx = gxp.tile([P, NG, 256, 4], BF16, name="gx", align_bytes=64)
            gxw = gx[:].bitcast(F32)
            for g in range(NG):
                tp = transposes(src, g)
                nc.scalar.copy(out=gxw[:, g, :, :], in_=tp[:].rearrange("p u a r -> p (a r) u"))
            nc.vector.quantize_mx(
                out=xc[:, c, :, :].rearrange("p g j -> p (g j)").bitcast(FP8X4),
                scales=xs[:, c, :, :].rearrange("p g j -> p (g j)"),
                in_=gx[:].rearrange("p g j t -> p (g j t)"),
            )
            for a in range(2):
                jx = jkp.tile([P, DIN], BF16, name="jx", tag="jx", bufs=2)
                nc.scalar.activation(out=jx[:], in_=src[:, a, :], func=ACT.Square,
                                     accum_out=xn2[:, 2 * c + a:2 * c + a + 1])

        def w_pair(c, src):
            gw = gwp.tile([P, NG, 256, 4], BF16, name="gw", align_bytes=64)
            for g in range(NG):
                tp = transposes(src, g)
                nc.vector.tensor_scalar(
                    out=gw[:, g, :, :].rearrange("p j (u e) -> p j u e", e=2),
                    in0=tp[:].bitcast(BF16).rearrange("p u a (r e) -> p (a r) u e", e=2),
                    scalar1=0.1, scalar2=None, op0=ALU.mult,
                )
            for g in range(NG):
                nc.vector.quantize_mx(
                    out=wc[:, g, 256 * c:256 * c + 256].bitcast(FP8X4),
                    scales=ws[:, g, 256 * c:256 * c + 256],
                    in_=gw[:, g, :, :].rearrange("p j t -> p (j t)"),
                )

        banks = {}

        def mx_block(r, n):
            acc = psum.tile([P, 512], F32, tag="bk%d" % (4 * (r % 2) + n), name="acc")
            banks[(r, n)] = acc
            c, a = r // 2, r % 2
            for g in range(NG):
                nc.tensor.matmul_mx(
                    out=acc[:],
                    lhsT=xc[:, c, g, 128 * a:128 * a + 128].bitcast(FP8X4),
                    lhsT_scale=xs[:, c, g, 128 * a:128 * a + 128],
                    rhs=wc[:, g, 512 * n:512 * n + 512].bitcast(FP8X4),
                    rhs_scale=ws[:, g, 512 * n:512 * n + 512],
                    start=(g == 0), stop=(g == NG - 1),
                )

        def load(pool, view, c, nm):
            t = pool.tile([P, 2, DIN], BF16, name=nm, tag=nm)
            nc.sync.dma_start(out=t[:], in_=view[c])
            return t

        order = [("x", 0), ("w", 0), ("w", 1), ("b", 0), ("x", 1), ("w", 2), ("w", 3),
                 ("x", 2), ("w", 4), ("w", 5), ("x", 3), ("w", 6), ("w", 7)]
        loaded = {}
        for kind, c in order:
            if kind == "x":
                loaded[(kind, c)] = load(xin, x_v, c, "xt")
            elif kind == "w":
                loaded[(kind, c)] = load(win, w_v, c, "wt")
            else:
                nc.sync.dma_start(out=bias_bc[:], in_=bias.partition_broadcast(P))

        def xn_batch():
            xc2 = sm.tile([P, NT], F32, name="xc2", bufs=1)
            nc.gpsimd.tensor_scalar(out=xc2[:], in0=xn2[:], scalar1=1e-30, scalar2=None, op0=ALU.max)
            rxn = sm.tile([P, NT], F32, name="rxn", bufs=1)
            nc.gpsimd.tensor_tensor(out=rxn[:], in0=xc2[:], in1=mh8[:], op=ALU.pow)
            v = sm.tile([P, NT], F32, name="v", bufs=1)
            nc.vector.tensor_tensor(out=v[:], in0=xc2[:], in1=rxn[:], op=ALU.mult)
            nc.vector.tensor_scalar(out=v[:], in0=v[:], scalar1=1.0 - 1e-5, scalar2=None, op0=ALU.min)
            l1 = sm.tile([P, NT], F32, name="l1", bufs=1)
            l2 = sm.tile([P, NT], F32, name="l2", bufs=1)
            nc.scalar.activation(out=l1[:], in_=v[:], func=ACT.Ln, bias=1.0, scale=1.0)
            nc.scalar.activation(out=l2[:], in_=v[:], func=ACT.Ln, bias=1.0, scale=-1.0)
            nc.vector.tensor_tensor(out=l1[:], in0=l1[:], in1=l2[:], op=ALU.subtract)
            nc.vector.scalar_tensor_tensor(out=q[:], in0=l1[:], scalar=0.5, in1=rxn[:],
                                           op0=ALU.mult, op1=ALU.mult)

        def bias_map():
            sb = sm.tile([P, 1], F32, name="sb", bufs=1)
            nc.scalar.activation(out=b_bc[:], in_=bias_bc[:], func=ACT.Square, accum_out=sb[:])
            u2 = sm.tile([P, 1], F32, name="u2", bufs=1)
            nc.gpsimd.tensor_scalar(out=u2[:], in0=sb[:], scalar1=0.01, scalar2=1e-30,
                                    op0=ALU.mult, op1=ALU.max)
            run = sm.tile([P, 1], F32, name="run", bufs=1)
            nc.gpsimd.tensor_tensor(out=run[:], in0=u2[:], in1=mh8[:, 0:1], op=ALU.pow)
            tb = sm.tile([P, 1], F32, name="tb", bufs=1)
            nc.scalar.activation(out=tb[:], in_=u2[:], func=ACT.Tanh, scale=run[:, 0:1])
            scb = sm.tile([P, 1], F32, name="scb", bufs=1)
            nc.vector.tensor_scalar(out=scb[:], in0=tb[:], scalar1=run[:, 0:1], scalar2=0.1,
                                    op0=ALU.mult, op1=ALU.mult)
            nc.vector.tensor_tensor(out=y2[:], in0=tb[:], in1=tb[:], op=ALU.mult)
            nc.vector.tensor_scalar(out=c2[:], in0=y2[:], scalar1=-1.0, scalar2=None, op0=ALU.add)
            nc.vector.tensor_scalar(out=b_bc[:], in0=bias_bc[:], scalar1=scb[:, 0:1], scalar2=None,
                                    op0=ALU.mult)

        for kind, c in order:
            if kind == "x":
                x_pair(c, loaded[(kind, c)])
                if c == 3:
                    xn_batch()
                    bias_map()
            elif kind == "w":
                w_pair(c, loaded[(kind, c)])
                if c % 2 == 1:
                    mx_block(0, c // 2)

        sums = {}
        coef = {}
        tts = {}

        def sums_of(r):
            ssq = sm.tile([P, NB], F32, name="ssq")
            dot = sm.tile([P, NB], F32, name="dot")
            sums[r] = (ssq, dot)
            for n in range(NB):
                acc = banks[(r, n)]
                jk = jkp.tile([P, 512], F32, name="jk", tag="jk")
                nc.scalar.activation(out=jk[:], in_=acc[:], func=ACT.Square,
                                     accum_out=ssq[:, n:n + 1])
                nc.vector.scalar_tensor_tensor(out=jk[:], in0=acc[:], scalar=2.0,
                                               in1=b_bc[:, 512 * n:512 * n + 512],
                                               op0=ALU.mult, op1=ALU.mult,
                                               accum_out=dot[:, n:n + 1])

        def col(nm):
            return sm.tile([P, 1], F32, name=nm, tag=nm)

        def chain_stages(r):
            ssq, dot = sums[r]
            ce = nc.vector
            loc = {}

            def st_a():
                y = col("y")
                nc.vector.tensor_reduce(out=y[:], in_=ssq[:], axis=AX.X, op=ALU.add)
                d2 = col("d2")
                nc.vector.tensor_reduce(out=d2[:], in_=dot[:], axis=AX.X, op=ALU.add)
                yc = col("yc")
                nc.gpsimd.tensor_scalar(out=yc[:], in0=y[:], scalar1=1e-30, scalar2=None, op0=ALU.max)
                rmn = col("rmn")
                nc.gpsimd.tensor_tensor(out=rmn[:], in0=yc[:], in1=mh8[:, 0:1], op=ALU.pow)
                sq = col("sq")
                nc.gpsimd.tensor_scalar(out=sq[:], in0=rmn[:], scalar1=q[:, r:r + 1], scalar2=None,
                                        op0=ALU.mult)
                th = col("th")
                nc.scalar.activation(out=th[:], in_=yc[:], func=ACT.Tanh, scale=sq[:, 0:1])
                loc["d2"], loc["rmn"], loc["th"] = d2, rmn, th

            def st_b():
                th, rmn, d2 = loc["th"], loc["rmn"], loc["d2"]
                s = col("s")
                ce.tensor_scalar(out=s[:], in0=th[:], scalar1=rmn[:, 0:1], scalar2=None, op0=ALU.mult)
                x2 = col("x2")
                ce.tensor_scalar(out=x2[:], in0=th[:], scalar1=th[:, 0:1], scalar2=None, op0=ALU.mult)
                e1 = col("e1")
                ce.tensor_scalar(out=e1[:], in0=s[:], scalar1=d2[:, 0:1], scalar2=1.0,
                                 op0=ALU.mult, op1=ALU.add)
                pk = sm.tile([P, 2], F32, name="pk", tag="pk")
                den = col("den")
                ce.tensor_scalar(out=den[:], in0=x2[:], scalar1=y2[:, 0:1], scalar2=e1[:, 0:1],
                                 op0=ALU.mult, op1=ALU.add)
                num = col("num")
                ce.tensor_scalar(out=num[:], in0=x2[:], scalar1=c2[:, 0:1], scalar2=e1[:, 0:1],
                                 op0=ALU.add, op1=ALU.add)
                ce.tensor_scalar(out=pk[:, 0:1], in0=den[:], scalar1=1e-15, scalar2=None, op0=ALU.max)
                ce.tensor_scalar(out=pk[:, 1:2], in0=num[:], scalar1=pk[:, 0:1], scalar2=1e-30,
                                 op0=ALU.mult, op1=ALU.max)
                pw = sm.tile([P, 2], F32, name="pw", tag="pw")
                nc.gpsimd.tensor_tensor(out=pw[:], in0=pk[:], in1=ex2[:], op=ALU.pow)
                asx = col("asx")
                ce.tensor_scalar(out=asx[:], in0=e1[:], scalar1=y2[:, 0:1], scalar2=s[:, 0:1],
                                 op0=ALU.add, op1=ALU.mult)
                bc = col("bc")
                ce.tensor_scalar(out=bc[:], in0=x2[:], scalar1=-1.0, scalar2=1.0,
                                 op0=ALU.mult, op1=ALU.add)
                loc["pw"], loc["asx"], loc["bc"] = pw, asx, bc

            def st_c():
                pw, asx, bc = loc["pw"], loc["asx"], loc["bc"]
                pr = col("pr")
                ce.tensor_scalar(out=pr[:], in0=pw[:, 1:2], scalar1=0.999, scalar2=pw[:, 0:1],
                                 op0=ALU.mult, op1=ALU.min)
                al = col("al")
                ce.tensor_scalar(out=al[:], in0=asx[:], scalar1=pr[:, 0:1], scalar2=None, op0=ALU.mult)
                be = col("be")
                ce.tensor_scalar(out=be[:], in0=bc[:], scalar1=pr[:, 0:1], scalar2=None, op0=ALU.mult)
                coef[r] = (al, be)

            return [st_a, st_b, st_c]

        def scale_rows(r):
            al, be = coef[r]
            t = tpl.tile([P, DOUT], F32, name="t", tag="t")
            tts[r] = t
            for n in range(NB):
                nc.scalar.activation(out=t[:, 512 * n:512 * n + 512], in_=banks[(r, n)][:],
                                     func=ACT.Copy, scale=al[:, 0:1])

        def add_bias(r, h):
            al, be = coef[r]
            t = tts[r]
            sl = slice(1024 * h, 1024 * h + 1024)
            nc.vector.scalar_tensor_tensor(out=t[:, sl], in0=b_bc[:, sl], scalar=be[:, 0:1],
                                           in1=t[:, sl], op0=ALU.mult, op1=ALU.add)

        def leaky_store(r, h):
            t = tts[r]
            sl = slice(1024 * h, 1024 * h + 1024)
            nc.vector.scalar_tensor_tensor(out=t[:, sl], in0=t[:, sl], scalar=0.2,
                                           in1=t[:, sl], op0=ALU.mult, op1=ALU.max)
            nc.sync.dma_start(out=out_v[r][:, sl], in_=t[:, sl])

        for r in range(NT + 1):
            if r < NT:
                if r > 0:
                    for n in range(NB):
                        mx_block(r, n)
                sums_of(r)
            stages = chain_stages(r) if r < NT else []
            if r > 0:
                scale_rows(r - 1)
            big = []
            if r > 0:
                big = [lambda: add_bias(r - 1, 0), lambda: add_bias(r - 1, 1),
                       lambda: leaky_store(r - 1, 0), lambda: leaky_store(r - 1, 1)]
            for i in range(4):
                if i < len(stages):
                    stages[i]()
                if i < len(big):
                    big[i]()
